import numpy as np
import ml_dtypes


def mxq(x, axis, fmt="e4m3"):
    dtype, down = {"e4m3": (ml_dtypes.float8_e4m3fn, 7), "e5m2": (ml_dtypes.float8_e5m2, 14)}[fmt]
    v = np.moveaxis(np.asarray(x, np.float32).astype(ml_dtypes.bfloat16).astype(np.float64), axis, -1)
    blocks = v.reshape(v.shape[:-1] + (-1, 32))
    amax = np.abs(blocks).max(-1, keepdims=True)
    byte = np.maximum(np.where(amax > 0, np.frexp(amax)[1] - 1 + 127, 0) - down, 1)
    scale = np.exp2(byte - 127.0)
    codes = (blocks / scale).astype(np.float32).astype(dtype).astype(np.float64)
    return np.moveaxis((codes * scale).reshape(v.shape), -1, axis)


WIDE = False


def mx_kscale(k):
    if not WIDE:
        return np.ones(k)
    levels = np.array([10, -10, 5, -5, 0])
    a = np.random.permutation(np.resize(levels, k // 512 * 4)).reshape(k // 512, 4)
    idx = np.arange(k)
    return np.exp2(a[idx // 512, idx % 128 // 32])


BF16 = ml_dtypes.bfloat16


def bf(x):
    return np.asarray(x, np.float32).astype(BF16)


def f64(x):
    return np.asarray(x).astype(np.float64)


B, N, D, H, S = 4, 1024, 1024, 384, 256
E = 2 * H + S
EPS = 1e-5


def silu(z):
    return z / (1.0 + np.exp(-z))


def setup_inputs():
    s = mx_kscale(D)
    c = np.exp2(np.round(np.log2(np.sqrt(np.mean(s * s)))))
    rows = np.exp(0.5 * np.random.standard_normal((B, N, 1)))
    return {"x": bf(np.random.standard_normal((B, N, D)) * rows * s),
            "g": bf(1.3 + 0.05 * np.random.standard_normal(1)),
            "W_uv": bf(np.random.standard_normal((D, E)) * 0.55 / np.sqrt(D) / s[:, None] * c),
            "b_uv": bf(0.1 * np.random.standard_normal(E)),
            "gamma": bf(1.0 + 0.1 * np.random.standard_normal((2, S))),
            "beta": bf(0.1 * np.random.standard_normal((2, S)))}


def reference(x, g, W_uv, b_uv, gamma, beta):
    x, g, gamma, beta = f64(x), f64(g), f64(gamma), f64(beta)
    norm = np.sqrt((x * x).sum(-1, keepdims=True)) * (1.0 / np.sqrt(D))
    xn = x / np.maximum(norm, EPS) * g
    uv = silu((mxq(xn, 2, "e4m3") @ mxq(f64(W_uv), 0, "e4m3")) + f64(b_uv))
    u = uv[..., :H]
    v = uv[..., H:2 * H]
    base = uv[..., 2 * H:]
    q = base * gamma[0] + beta[0]
    k = base * gamma[1] + beta[1]
    return u, v, q, k

@@ -1,0 +1,260 @@
+from contextlib import ExitStack
+
+import concourse.mybir as mybir
+from concourse.masks import make_identity
+
+F32 = mybir.dt.float32
+BF16 = mybir.dt.bfloat16
+U32 = mybir.dt.uint32
+U8 = mybir.dt.uint8
+FP8X4 = mybir.dt.float8_e4m3fn_x4
+ACT = mybir.ActivationFunctionType
+ALU = mybir.AluOpType
+
+P = 128
+TOKENS = 4 * 1024
+D = 1024
+H = 384
+S = 256
+E = 2 * H + S
+EPS = 1e-5
+
+K_PASS = 4 * P
+PASSES = D // K_PASS
+N_BANK = 512
+BANKS = E // N_BANK
+WORDS = D // 2
+
+T = 4
+GROUP = T * P
+GROUPS = TOKENS // GROUP
+TILES = TOKENS // P
+RUN = 2
+
+FLOPS = 2 * TOKENS * D * E
+
+
+def tile_gatedattentionunit_pa_t_kernel(
+    tc, x, g, W_uv, b_uv, gamma, beta, out_0, out_1, out_2, out_3
+):
+    nc = tc.nc
+    x_rows = x.flatten_outer_dims()
+    u_rows = out_0.flatten_outer_dims()
+    v_rows = out_1.flatten_outer_dims()
+    q_rows = out_2.flatten_outer_dims()
+    k_rows = out_3.flatten_outer_dims()
+
+    with ExitStack() as stack:
+        const = stack.enter_context(tc.tile_pool(name="const", bufs=1))
+        x_pool = stack.enter_context(tc.tile_pool(name="x_pool", bufs=1))
+        w_stage = stack.enter_context(tc.tile_pool(name="w_stage", bufs=2))
+        front = stack.enter_context(tc.tile_pool(name="front", bufs=4))
+        back = stack.enter_context(tc.tile_pool(name="back", bufs=4))
+        outs = stack.enter_context(tc.tile_pool(name="outs", bufs=2))
+        psum_t = stack.enter_context(tc.psum_pool(name="psum_t", bufs=4))
+        psum_acc = stack.enter_context(tc.psum_pool(name="psum_acc", bufs=4))
+
+        def load_x(grp):
+            x_grp = x_pool.tile([P, T, D], BF16, name="x_grp%d" % grp)
+            nc.sync.dma_start(
+                out=x_grp[:],
+                in_=x_rows[grp * GROUP : (grp + 1) * GROUP, :].rearrange(
+                    "(p t) d -> p t d", t=T
+                ),
+            )
+            return x_grp
+
+        g_bf = const.tile([P, 1], BF16)
+        nc.sync.dma_start(out=g_bf[:], in_=g.partition_broadcast(P))
+        const_rows = const.tile([P, 4 * N_BANK], BF16)
+        nc.vector.memset(const_rows[:], 0.0)
+        nc.sync.dma_start(out=const_rows[0:1, 0:E], in_=b_uv.unsqueeze(0))
+        nc.sync.dma_start(
+            out=const_rows[0:1, E : E + 2 * S],
+            in_=gamma.rearrange("a s -> (a s)").unsqueeze(0),
+        )
+        nc.sync.dma_start(
+            out=const_rows[0:1, E + 2 * S : E + 4 * S],
+            in_=beta.rearrange("a s -> (a s)").unsqueeze(0),
+        )
+        x_sb = [load_x(0)]
+        w_raw = const.tile([P, PASSES, 4, E], BF16)
+        for c in range(PASSES):
+            nc.sync.dma_start(
+                out=w_raw[:, c, :, :].rearrange("p (u e) n -> p u e n", e=2),
+                in_=W_uv[c * K_PASS : (c + 1) * K_PASS, :].rearrange(
+                    "(u p e) n -> p u e n", u=2, e=2
+                ),
+            )
+        for grp in range(1, GROUPS):
+            x_sb.append(load_x(grp))
+
+        ident = const.tile([P, P], F32)
+        make_identity(nc, ident[:])
+        neg_half = const.tile([P, 1], F32)
+        nc.gpsimd.memset(neg_half[:], -0.5)
+        g_f32 = const.tile([P, 1], F32)
+        nc.vector.tensor_copy(out=g_f32[:], in_=g_bf[:])
+        warm = const.tile([P, 1], F32)
+        nc.vector.memset(warm[:], 0.0)
+        nc.scalar.activation(out=warm[:], in_=warm[:], func=ACT.Silu)
+
+        ones = const.tile([P, P], BF16)
+        nc.vector.memset(ones[:], 1.0)
+        const_bc = const.tile([P, 4 * N_BANK], F32)
+        for n in range(4):
+            cols = slice(n * N_BANK, (n + 1) * N_BANK)
+            spread = psum_acc.tile([P, N_BANK], F32, name="acc")
+            nc.tensor.matmul(
+                out=spread[:], lhsT=ones[:], rhs=const_rows[:, cols], start=True, stop=True
+            )
+            nc.vector.tensor_copy(out=const_bc[:, cols], in_=spread[:])
+        bias_bc = const_bc[:, 0:E]
+        gamma_bc = const_bc[:, E : E + 2 * S].rearrange("p (a s) -> p a s", a=2)
+        beta_bc = const_bc[:, E + 2 * S : E + 4 * S].rearrange("p (a s) -> p a s", a=2)
+
+        w_codes = const.tile([P, PASSES, E], U32, align_bytes=64)
+        w_scales = const.tile([P, PASSES, E], U8, align_bytes=64)
+        for c in range(PASSES):
+            for n in range(BANKS):
+                cols = slice(n * N_BANK, (n + 1) * N_BANK)
+                w_grouped = w_stage.tile([P, N_BANK, 4], BF16, align_bytes=64)
+                nc.vector.tensor_copy(
+                    out=w_grouped[:].rearrange("p (n i) j -> p n j i", i=4),
+                    in_=w_raw[:, c, :, cols].rearrange("p j (n i) -> p n j i", i=4),
+                )
+                nc.vector.quantize_mx(
+                    out=w_codes[:, c, cols].bitcast(FP8X4),
+                    scales=w_scales[:, c, cols],
+                    in_=w_grouped[:].rearrange("p n j -> p (n j)"),
+                )
+
+        sumsq = const.tile([P, TILES], F32)
+        meansq = const.tile([P, TILES], F32)
+        rnorm = const.tile([P, TILES], F32)
+        codes = {}
+        scales = {}
+        group_out = {}
+
+        def x_tile(i):
+            return x_sb[i // T][:, i % T, :]
+
+        def norm(i):
+            col = slice(i, i + 1)
+            squares = front.tile([P, D], BF16)
+            nc.scalar.activation(
+                out=squares[:], in_=x_tile(i), func=ACT.Square, accum_out=sumsq[:, col]
+            )
+            nc.gpsimd.tensor_scalar(
+                out=meansq[:, col],
+                in0=sumsq[:, col],
+                scalar1=1.0 / D,
+                scalar2=EPS * EPS,
+                op0=ALU.mult,
+                op1=ALU.max,
+            )
+            nc.gpsimd.tensor_tensor(
+                out=rnorm[:, col], in0=meansq[:, col], in1=neg_half[:], op=ALU.pow
+            )
+
+        def transpose(i):
+            xn = front.tile([P, D], BF16)
+            nc.vector.tensor_scalar(
+                out=xn[:],
+                in0=x_tile(i),
+                scalar1=rnorm[:, i : i + 1],
+                scalar2=g_f32[:],
+                op0=ALU.mult,
+                op1=ALU.mult,
+            )
+            xn_words = xn[:].bitcast(F32)
+            xt = psum_t.tile([P, WORDS // P, P], F32)
+            for j in range(WORDS // P):
+                nc.tensor.transpose(xt[:, j, :], xn_words[:, j * P : (j + 1) * P], ident[:])
+            grouped = front.tile([P, D], BF16, align_bytes=64)
+            nc.scalar.copy(
+                out=grouped[:].bitcast(F32).rearrange("p (c r u) -> p c r u", c=PASSES, u=2),
+                in_=xt[:].rearrange("p (c u) r -> p c r u", u=2),
+            )
+            return grouped
+
+        def quantise(i, grouped):
+            codes[i] = front.tile([P, PASSES * P], U32, name="codes", align_bytes=64)
+            scales[i] = front.tile([P, PASSES * P], U8, name="scales", align_bytes=64)
+            nc.vector.quantize_mx(
+                out=codes[i][:].bitcast(FP8X4), scales=scales[i][:], in_=grouped[:]
+            )
+
+        def project(i):
+            z = back.tile([P, E], F32)
+            for n in range(BANKS):
+                cols = slice(n * N_BANK, (n + 1) * N_BANK)
+                acc = psum_acc.tile([P, N_BANK], F32)
+                for c in range(PASSES):
+                    toks = slice(c * P, (c + 1) * P)
+                    nc.tensor.matmul_mx(
+                        out=acc[:],
+                        lhsT=codes[i][:, toks].bitcast(FP8X4),
+                        lhsT_scale=scales[i][:, toks],
+                        rhs=w_codes[:, c, cols].bitcast(FP8X4),
+                        rhs_scale=w_scales[:, c, cols],
+                        start=(c == 0),
+                        stop=(c == PASSES - 1),
+                    )
+                nc.vector.tensor_tensor(
+                    out=z[:, cols], in0=acc[:], in1=bias_bc[:, cols], op=ALU.add
+                )
+            return z
+
+        def finish(i, z):
+            grp, t = i // T, i % T
+            if t == 0:
+                group_out["u"] = outs.tile([P, T, H], F32, name="u_out")
+                group_out["v"] = outs.tile([P, T, H], F32, name="v_out")
+                group_out["qk"] = outs.tile([P, 2, T, S], F32, name="qk_out")
+            u_out, v_out, qk_out = group_out["u"], group_out["v"], group_out["qk"]
+            nc.scalar.activation(out=u_out[:, t, :], in_=z[:, 0:H], func=ACT.Silu)
+            nc.scalar.activation(out=v_out[:, t, :], in_=z[:, H : 2 * H], func=ACT.Silu)
+            base = back.tile([P, S], F32)
+            nc.scalar.activation(out=base[:], in_=z[:, 2 * H : E], func=ACT.Silu)
+            scaled = back.tile([P, 2, S], F32)
+            nc.vector.tensor_tensor(
+                out=scaled[:],
+                in0=base[:].unsqueeze(1).to_broadcast([P, 2, S]),
+                in1=gamma_bc,
+                op=ALU.mult,
+            )
+            nc.vector.tensor_tensor(
+                out=qk_out[:, :, t, :], in0=scaled[:], in1=beta_bc, op=ALU.add
+            )
+            if t == T - 1:
+                rows = slice(grp * GROUP, (grp + 1) * GROUP)
+                for dram, sbuf in (
+                    (u_rows, u_out[:]),
+                    (v_rows, v_out[:]),
+                    (q_rows, qk_out[:, 0, :, :]),
+                    (k_rows, qk_out[:, 1, :, :]),
+                ):
+                    nc.sync.dma_start(
+                        out=dram[rows, :].rearrange("(p t) n -> p t n", t=T), in_=sbuf
+                    )
+
+        def front_of(run):
+            tiles = range(run * RUN, (run + 1) * RUN)
+            for i in tiles:
+                norm(i)
+            grouped = [transpose(i) for i in tiles]
+            for i, grouped_i in zip(tiles, grouped):
+                quantise(i, grouped_i)
+
+        def back_of(run):
+            tiles = range(run * RUN, (run + 1) * RUN)
+            z = [project(i) for i in tiles]
+            for i, z_i in zip(tiles, z):
+                finish(i, z_i)
+
+        front_of(0)
+        for run in range(TILES // RUN):
+            if run + 1 < TILES // RUN:
+                front_of(run + 1)
+            back_of(run)

@@ -22,14 +22,17 @@ EPS = 1e-5
 K_PASS = 4 * P
 PASSES = D // K_PASS
 N_BANK = 512
-BANKS = E // N_BANK
-WORDS = D // 2
+N_TAIL = 2 * H - N_BANK
+WORD_BLOCKS = D // 2 // P
+BASE_BLOCKS = S // P
 
 T = 4
 GROUP = T * P
 GROUPS = TOKENS // GROUP
 TILES = TOKENS // P
 RUN = 2
+RUN_TOKENS = RUN * P
+RUNS = TILES // RUN
 
 FLOPS = 2 * TOKENS * D * E
 
@@ -48,11 +51,13 @@ def tile_gatedattentionunit_pa_t_kernel(
         const = stack.enter_context(tc.tile_pool(name="const", bufs=1))
         x_pool = stack.enter_context(tc.tile_pool(name="x_pool", bufs=1))
         w_stage = stack.enter_context(tc.tile_pool(name="w_stage", bufs=2))
-        front = stack.enter_context(tc.tile_pool(name="front", bufs=4))
-        back = stack.enter_context(tc.tile_pool(name="back", bufs=4))
+        front = stack.enter_context(tc.tile_pool(name="front", bufs=3))
+        back = stack.enter_context(tc.tile_pool(name="back", bufs=3))
         outs = stack.enter_context(tc.tile_pool(name="outs", bufs=2))
         psum_t = stack.enter_context(tc.psum_pool(name="psum_t", bufs=4))
-        psum_acc = stack.enter_context(tc.psum_pool(name="psum_acc", bufs=4))
+        psum_head = stack.enter_context(tc.psum_pool(name="psum_head", bufs=2))
+        psum_tail = stack.enter_context(tc.psum_pool(name="psum_tail", bufs=1))
+        psum_base = stack.enter_context(tc.psum_pool(name="psum_base", bufs=1))
 
         def load_x(grp):
             x_grp = x_pool.tile([P, T, D], BF16, name="x_grp%d" % grp)
@@ -66,16 +71,19 @@ def tile_gatedattentionunit_pa_t_kernel(
 
         g_bf = const.tile([P, 1], BF16)
         nc.sync.dma_start(out=g_bf[:], in_=g.partition_broadcast(P))
-        const_rows = const.tile([P, 4 * N_BANK], BF16)
-        nc.vector.memset(const_rows[:], 0.0)
-        nc.sync.dma_start(out=const_rows[0:1, 0:E], in_=b_uv.unsqueeze(0))
+        uv_bias_row = const.tile([P, 2 * H], BF16)
+        nc.vector.memset(uv_bias_row[:], 0.0)
+        nc.sync.dma_start(out=uv_bias_row[0:1, :], in_=b_uv[0 : 2 * H].unsqueeze(0))
+        base_rows = const.tile([P, P], BF16)
+        nc.vector.memset(base_rows[:], 0.0)
         nc.sync.dma_start(
-            out=const_rows[0:1, E : E + 2 * S],
-            in_=gamma.rearrange("a s -> (a s)").unsqueeze(0),
+            out=base_rows[0:2, :], in_=b_uv[2 * H : E].rearrange("(b n) -> b n", n=P)
         )
         nc.sync.dma_start(
-            out=const_rows[0:1, E + 2 * S : E + 4 * S],
-            in_=beta.rearrange("a s -> (a s)").unsqueeze(0),
+            out=base_rows[2:6, :], in_=gamma.rearrange("a (b n) -> (a b) n", n=P)
+        )
+        nc.sync.dma_start(
+            out=base_rows[6:10, :], in_=beta.rearrange("a (b n) -> (a b) n", n=P)
         )
         x_sb = [load_x(0)]
         w_raw = const.tile([P, PASSES, 4, E], BF16)
@@ -91,7 +99,9 @@ def tile_gatedattentionunit_pa_t_kernel(
 
         ident = const.tile([P, P], F32)
         make_identity(nc, ident[:])
-        neg_half = const.tile([P, 1], F32)
+        ident_bf = const.tile([P, P], BF16)
+        make_identity(nc, ident_bf[:])
+        neg_half = const.tile([P, RUN], F32)
         nc.gpsimd.memset(neg_half[:], -0.5)
         g_f32 = const.tile([P, 1], F32)
         nc.vector.tensor_copy(out=g_f32[:], in_=g_bf[:])
@@ -101,22 +111,37 @@ def tile_gatedattentionunit_pa_t_kernel(
 
         ones = const.tile([P, P], BF16)
         nc.vector.memset(ones[:], 1.0)
-        const_bc = const.tile([P, 4 * N_BANK], F32)
-        for n in range(4):
-            cols = slice(n * N_BANK, (n + 1) * N_BANK)
-            spread = psum_acc.tile([P, N_BANK], F32, name="acc")
+        uv_bias = const.tile([P, 2 * H], F32)
+        for first, width in ((0, N_BANK), (N_BANK, N_TAIL)):
+            spread = psum_head.tile([P, N_BANK], F32, name="head")
             nc.tensor.matmul(
-                out=spread[:], lhsT=ones[:], rhs=const_rows[:, cols], start=True, stop=True
+                out=spread[:, 0:width],
+                lhsT=ones[:],
+                rhs=uv_bias_row[:, first : first + width],
+                start=True,
+                stop=True,
             )
-            nc.vector.tensor_copy(out=const_bc[:, cols], in_=spread[:])
-        bias_bc = const_bc[:, 0:E]
-        gamma_bc = const_bc[:, E : E + 2 * S].rearrange("p (a s) -> p a s", a=2)
-        beta_bc = const_bc[:, E + 2 * S : E + 4 * S].rearrange("p (a s) -> p a s", a=2)
+            nc.vector.tensor_copy(
+                out=uv_bias[:, first : first + width], in_=spread[:, 0:width]
+            )
+        base_cols_ps = psum_t.tile([P, P], BF16, name="bank_t")
+        nc.tensor.transpose(base_cols_ps[:], base_rows[:], ident_bf[:])
+        base_cols = const.tile([P, 10], F32)
+        nc.vector.tensor_copy(out=base_cols[:], in_=base_cols_ps[:, 0:10])
+
+        def base_bias(b):
+            return base_cols[:, b : b + 1]
+
+        def base_gamma(a, b):
+            return base_cols[:, 2 + 2 * a + b : 3 + 2 * a + b]
+
+        def base_beta(a, b):
+            return base_cols[:, 6 + 2 * a + b : 7 + 2 * a + b]
 
         w_codes = const.tile([P, PASSES, E], U32, align_bytes=64)
         w_scales = const.tile([P, PASSES, E], U8, align_bytes=64)
         for c in range(PASSES):
-            for n in range(BANKS):
+            for n in range(E // N_BANK):
                 cols = slice(n * N_BANK, (n + 1) * N_BANK)
                 w_grouped = w_stage.tile([P, N_BANK, 4], BF16, align_bytes=64)
                 nc.vector.tensor_copy(
@@ -132,129 +157,201 @@ def tile_gatedattentionunit_pa_t_kernel(
         sumsq = const.tile([P, TILES], F32)
         meansq = const.tile([P, TILES], F32)
         rnorm = const.tile([P, TILES], F32)
-        codes = {}
-        scales = {}
+        x_banks = {}
+        x_codes = {}
+        x_scales = {}
+        qk_t = {}
+        qk_banks = {}
         group_out = {}
 
         def x_tile(i):
             return x_sb[i // T][:, i % T, :]
 
-        def norm(i):
-            col = slice(i, i + 1)
-            squares = front.tile([P, D], BF16)
-            nc.scalar.activation(
-                out=squares[:], in_=x_tile(i), func=ACT.Square, accum_out=sumsq[:, col]
-            )
+        def norm(r):
+            for i in range(r * RUN, (r + 1) * RUN):
+                squares = front.tile([P, D], BF16)
+                nc.scalar.activation(
+                    out=squares[:],
+                    in_=x_tile(i),
+                    func=ACT.Square,
+                    accum_out=sumsq[:, i : i + 1],
+                )
+            cols = slice(r * RUN, (r + 1) * RUN)
             nc.gpsimd.tensor_scalar(
-                out=meansq[:, col],
-                in0=sumsq[:, col],
+                out=meansq[:, cols],
+                in0=sumsq[:, cols],
                 scalar1=1.0 / D,
                 scalar2=EPS * EPS,
                 op0=ALU.mult,
                 op1=ALU.max,
             )
             nc.gpsimd.tensor_tensor(
-                out=rnorm[:, col], in0=meansq[:, col], in1=neg_half[:], op=ALU.pow
+                out=rnorm[:, cols], in0=meansq[:, cols], in1=neg_half[:], op=ALU.pow
             )
 
-        def transpose(i):
-            xn = front.tile([P, D], BF16)
-            nc.vector.tensor_scalar(
-                out=xn[:],
-                in0=x_tile(i),
-                scalar1=rnorm[:, i : i + 1],
-                scalar2=g_f32[:],
-                op0=ALU.mult,
-                op1=ALU.mult,
+        def transpose_x(r):
+            x_banks[r] = []
+            for i in range(r * RUN, (r + 1) * RUN):
+                xn = front.tile([P, D], BF16)
+                nc.vector.tensor_scalar(
+                    out=xn[:],
+                    in0=x_tile(i),
+                    scalar1=rnorm[:, i : i + 1],
+                    scalar2=g_f32[:],
+                    op0=ALU.mult,
+                    op1=ALU.mult,
+                )
+                xn_words = xn[:].bitcast(F32)
+                bank = psum_t.tile([P, WORD_BLOCKS, P], F32, name="bank_t")
+                for j in range(WORD_BLOCKS):
+                    nc.tensor.transpose(
+                        bank[:, j, :], xn_words[:, j * P : (j + 1) * P], ident[:]
+                    )
+                x_banks[r].append(bank)
+
+        def copy_out_x(r):
+            grouped = front.tile([P, PASSES * RUN_TOKENS * 4], BF16, align_bytes=64)
+            words = grouped[:].bitcast(F32).rearrange(
+                "p (c s r u) -> p c s r u", c=PASSES, s=RUN, u=2
             )
-            xn_words = xn[:].bitcast(F32)
-            xt = psum_t.tile([P, WORDS // P, P], F32)
-            for j in range(WORDS // P):
-                nc.tensor.transpose(xt[:, j, :], xn_words[:, j * P : (j + 1) * P], ident[:])
-            grouped = front.tile([P, D], BF16, align_bytes=64)
-            nc.scalar.copy(
-                out=grouped[:].bitcast(F32).rearrange("p (c r u) -> p c r u", c=PASSES, u=2),
-                in_=xt[:].rearrange("p (c u) r -> p c r u", u=2),
-            )
+            for s, bank in enumerate(x_banks[r]):
+                nc.vector.tensor_copy(
+                    out=words[:, :, s, :, :],
+                    in_=bank[:].rearrange("p (c u) r -> p c r u", u=2),
+                )
             return grouped
 
-        def quantise(i, grouped):
-            codes[i] = front.tile([P, PASSES * P], U32, name="codes", align_bytes=64)
-            scales[i] = front.tile([P, PASSES * P], U8, name="scales", align_bytes=64)
+        def quantise_x(r, grouped):
+            x_codes[r] = front.tile(
+                [P, PASSES * RUN_TOKENS], U32, name="x_codes", align_bytes=64
+            )
+            x_scales[r] = front.tile(
+                [P, PASSES * RUN_TOKENS], U8, name="x_scales", align_bytes=64
+            )
             nc.vector.quantize_mx(
-                out=codes[i][:].bitcast(FP8X4), scales=scales[i][:], in_=grouped[:]
+                out=x_codes[r][:].bitcast(FP8X4), scales=x_scales[r][:], in_=grouped[:]
             )
 
-        def project(i):
-            z = back.tile([P, E], F32)
-            for n in range(BANKS):
-                cols = slice(n * N_BANK, (n + 1) * N_BANK)
-                acc = psum_acc.tile([P, N_BANK], F32)
-                for c in range(PASSES):
-                    toks = slice(c * P, (c + 1) * P)
-                    nc.tensor.matmul_mx(
-                        out=acc[:],
-                        lhsT=codes[i][:, toks].bitcast(FP8X4),
-                        lhsT_scale=scales[i][:, toks],
-                        rhs=w_codes[:, c, cols].bitcast(FP8X4),
-                        rhs_scale=w_scales[:, c, cols],
-                        start=(c == 0),
-                        stop=(c == PASSES - 1),
-                    )
-                nc.vector.tensor_tensor(
-                    out=z[:, cols], in0=acc[:], in1=bias_bc[:, cols], op=ALU.add
-                )
-            return z
+        def w_operand(c, first, width):
+            cols = slice(first, first + width)
+            return w_codes[:, c, cols], w_scales[:, c, cols]
 
-        def finish(i, z):
-            grp, t = i // T, i % T
-            if t == 0:
+        def x_operand(r, c, first, width):
+            cols = slice(c * RUN_TOKENS + first, c * RUN_TOKENS + first + width)
+            return x_codes[r][:, cols], x_scales[r][:, cols]
+
+        def mx_pass(out, c, stationary, moving):
+            nc.tensor.matmul_mx(
+                out=out,
+                lhsT=stationary[0].bitcast(FP8X4),
+                lhsT_scale=stationary[1],
+                rhs=moving[0].bitcast(FP8X4),
+                rhs_scale=moving[1],
+                start=(c == 0),
+                stop=(c == PASSES - 1),
+            )
+
+        def project_base(r):
+            base_ps = psum_base.tile([P, BASE_BLOCKS, RUN_TOKENS], F32)
+            for b in range(BASE_BLOCKS):
+                for c in range(PASSES):
+                    mx_pass(
+                        base_ps[:, b, :],
+                        c,
+                        w_operand(c, 2 * H + b * P, P),
+                        x_operand(r, c, 0, RUN_TOKENS),
+                    )
+            base_t = back.tile([P, BASE_BLOCKS, RUN_TOKENS], F32)
+            qk_t[r] = back.tile([P, 2, BASE_BLOCKS, RUN_TOKENS], F32, name="qk_t")
+            for b in range(BASE_BLOCKS):
+                nc.scalar.activation(
+                    out=base_t[:, b, :], in_=base_ps[:, b, :], func=ACT.Silu, bias=base_bias(b)
+                )
+                for a in range(2):
+                    nc.gpsimd.tensor_scalar(
+                        out=qk_t[r][:, a, b, :],
+                        in0=base_t[:, b, :],
+                        scalar1=base_gamma(a, b),
+                        scalar2=base_beta(a, b),
+                        op0=ALU.mult,
+                        op1=ALU.add,
+                    )
+
+        def project_uv(r):
+            grp, t0 = (r * RUN) // T, (r * RUN) % T
+            z = back.tile([P, RUN, 2 * H], F32)
+            tail = psum_tail.tile([P, RUN, N_TAIL], F32)
+            for s in range(RUN):
+                head = psum_head.tile([P, N_BANK], F32)
+                for out, first, width in ((head[:], 0, N_BANK), (tail[:, s, :], N_BANK, N_TAIL)):
+                    for c in range(PASSES):
+                        mx_pass(out, c, x_operand(r, c, s * P, P), w_operand(c, first, width))
+                nc.vector.tensor_tensor(
+                    out=z[:, s, 0:N_BANK], in0=head[:], in1=uv_bias[:, 0:N_BANK], op=ALU.add
+                )
+            nc.vector.tensor_tensor(
+                out=z[:, :, N_BANK : 2 * H],
+                in0=tail[:],
+                in1=uv_bias[:, N_BANK : 2 * H].unsqueeze(1).to_broadcast([P, RUN, N_TAIL]),
+                op=ALU.add,
+            )
+            if t0 == 0:
                 group_out["u"] = outs.tile([P, T, H], F32, name="u_out")
                 group_out["v"] = outs.tile([P, T, H], F32, name="v_out")
-                group_out["qk"] = outs.tile([P, 2, T, S], F32, name="qk_out")
-            u_out, v_out, qk_out = group_out["u"], group_out["v"], group_out["qk"]
-            nc.scalar.activation(out=u_out[:, t, :], in_=z[:, 0:H], func=ACT.Silu)
-            nc.scalar.activation(out=v_out[:, t, :], in_=z[:, H : 2 * H], func=ACT.Silu)
-            base = back.tile([P, S], F32)
-            nc.scalar.activation(out=base[:], in_=z[:, 2 * H : E], func=ACT.Silu)
-            scaled = back.tile([P, 2, S], F32)
-            nc.vector.tensor_tensor(
-                out=scaled[:],
-                in0=base[:].unsqueeze(1).to_broadcast([P, 2, S]),
-                in1=gamma_bc,
-                op=ALU.mult,
-            )
-            nc.vector.tensor_tensor(
-                out=qk_out[:, :, t, :], in0=scaled[:], in1=beta_bc, op=ALU.add
-            )
-            if t == T - 1:
-                rows = slice(grp * GROUP, (grp + 1) * GROUP)
-                for dram, sbuf in (
-                    (u_rows, u_out[:]),
-                    (v_rows, v_out[:]),
-                    (q_rows, qk_out[:, 0, :, :]),
-                    (k_rows, qk_out[:, 1, :, :]),
-                ):
+            rows = slice(grp * GROUP, (grp + 1) * GROUP)
+            for dram, sbuf, cols in (
+                (u_rows, group_out["u"], slice(0, H)),
+                (v_rows, group_out["v"], slice(H, 2 * H)),
+            ):
+                nc.scalar.activation(
+                    out=sbuf[:, t0 : t0 + RUN, :], in_=z[:, :, cols], func=ACT.Silu
+                )
+                if t0 + RUN == T:
                     nc.sync.dma_start(
-                        out=dram[rows, :].rearrange("(p t) n -> p t n", t=T), in_=sbuf
+                        out=dram[rows, :].rearrange("(p t) n -> p t n", t=T), in_=sbuf[:]
                     )
 
-        def front_of(run):
-            tiles = range(run * RUN, (run + 1) * RUN)
-            for i in tiles:
-                norm(i)
-            grouped = [transpose(i) for i in tiles]
-            for i, grouped_i in zip(tiles, grouped):
-                quantise(i, grouped_i)
+        def transpose_qk(r):
+            qk_banks[r] = []
+            for a in range(2):
+                bank = psum_t.tile([P, RUN, S], F32, name="bank_t")
+                for s in range(RUN):
+                    for b in range(BASE_BLOCKS):
+                        nc.tensor.transpose(
+                            bank[:, s, b * P : (b + 1) * P],
+                            qk_t[r][:, a, b, s * P : (s + 1) * P],
+                            ident[:],
+                        )
+                qk_banks[r].append(bank)
 
-        def back_of(run):
-            tiles = range(run * RUN, (run + 1) * RUN)
-            z = [project(i) for i in tiles]
-            for i, z_i in zip(tiles, z):
-                finish(i, z_i)
+        def copy_out_qk(r):
+            grp, t0 = (r * RUN) // T, (r * RUN) % T
+            if t0 == 0:
+                group_out["qk"] = outs.tile([P, 2, T, S], F32, name="qk_out")
+            qk_out = group_out["qk"]
+            nc.vector.tensor_copy(out=qk_out[:, 0, t0 : t0 + RUN, :], in_=qk_banks[r][0][:])
+            nc.scalar.copy(out=qk_out[:, 1, t0 : t0 + RUN, :], in_=qk_banks[r][1][:])
+            if t0 + RUN == T:
+                rows = slice(grp * GROUP, (grp + 1) * GROUP)
+                for a, dram in enumerate((q_rows, k_rows)):
+                    nc.sync.dma_start(
+                        out=dram[rows, :].rearrange("(p t) n -> p t n", t=T),
+                        in_=qk_out[:, a, :, :],
+                    )
 
-        front_of(0)
-        for run in range(TILES // RUN):
-            if run + 1 < TILES // RUN:
-                front_of(run + 1)
-            back_of(run)
+        for r in range(-2, RUNS + 1):
+            if 0 <= r + 2 < RUNS:
+                norm(r + 2)
+            if 0 <= r + 1 < RUNS:
+                transpose_x(r + 1)
+            if 0 <= r - 1 < RUNS:
+                transpose_qk(r - 1)
+            if 0 <= r + 1 < RUNS:
+                grouped = copy_out_x(r + 1)
+            if 0 <= r - 1 < RUNS:
+                copy_out_qk(r - 1)
+            if 0 <= r + 1 < RUNS:
+                quantise_x(r + 1, grouped)
+            if 0 <= r < RUNS:
+                project_base(r)
+                project_uv(r)

@@ -26,9 +26,6 @@ N_TAIL = 2 * H - N_BANK
 WORD_BLOCKS = D // 2 // P
 BASE_BLOCKS = S // P
 
-T = 4
-GROUP = T * P
-GROUPS = TOKENS // GROUP
 TILES = TOKENS // P
 RUN = 2
 RUN_TOKENS = RUN * P
@@ -50,24 +47,29 @@ def tile_gatedattentionunit_pa_t_kernel(
     with ExitStack() as stack:
         const = stack.enter_context(tc.tile_pool(name="const", bufs=1))
         x_pool = stack.enter_context(tc.tile_pool(name="x_pool", bufs=1))
-        w_stage = stack.enter_context(tc.tile_pool(name="w_stage", bufs=2))
-        front = stack.enter_context(tc.tile_pool(name="front", bufs=3))
+        w_stage = stack.enter_context(tc.tile_pool(name="w_stage", bufs=4))
+        front = stack.enter_context(tc.tile_pool(name="front", bufs=4))
         back = stack.enter_context(tc.tile_pool(name="back", bufs=3))
-        outs = stack.enter_context(tc.tile_pool(name="outs", bufs=2))
+        outs = stack.enter_context(tc.tile_pool(name="outs", bufs=4))
         psum_t = stack.enter_context(tc.psum_pool(name="psum_t", bufs=4))
         psum_head = stack.enter_context(tc.psum_pool(name="psum_head", bufs=2))
         psum_tail = stack.enter_context(tc.psum_pool(name="psum_tail", bufs=1))
         psum_base = stack.enter_context(tc.psum_pool(name="psum_base", bufs=1))
+        stack.enter_context(tc.manual_schedule())
 
-        def load_x(grp):
-            x_grp = x_pool.tile([P, T, D], BF16, name="x_grp%d" % grp)
-            nc.sync.dma_start(
-                out=x_grp[:],
-                in_=x_rows[grp * GROUP : (grp + 1) * GROUP, :].rearrange(
-                    "(p t) d -> p t d", t=T
-                ),
+        def run_rows(dram, r):
+            return dram[r * RUN_TOKENS : (r + 1) * RUN_TOKENS, :].rearrange(
+                "(p s) n -> p s n", s=RUN
             )
-            return x_grp
+
+        def load_x(r):
+            x_run = x_pool.tile([P, RUN, D], BF16, name="x_run%d" % r)
+            nc.sync.dma_start(out=x_run[:], in_=run_rows(x_rows, r))
+            return x_run
+
+        warm = const.tile([P, 1], F32)
+        nc.vector.memset(warm[:], 0.0)
+        nc.scalar.activation(out=warm[:], in_=warm[:], func=ACT.Silu)
 
         g_bf = const.tile([P, 1], BF16)
         nc.sync.dma_start(out=g_bf[:], in_=g.partition_broadcast(P))
@@ -94,8 +96,8 @@ def tile_gatedattentionunit_pa_t_kernel(
                     "(u p e) n -> p u e n", u=2, e=2
                 ),
             )
-        for grp in range(1, GROUPS):
-            x_sb.append(load_x(grp))
+        for r in range(1, RUNS):
+            x_sb.append(load_x(r))
 
         ident = const.tile([P, P], F32)
         make_identity(nc, ident[:])
@@ -105,9 +107,6 @@ def tile_gatedattentionunit_pa_t_kernel(
         nc.gpsimd.memset(neg_half[:], -0.5)
         g_f32 = const.tile([P, 1], F32)
         nc.vector.tensor_copy(out=g_f32[:], in_=g_bf[:])
-        warm = const.tile([P, 1], F32)
-        nc.vector.memset(warm[:], 0.0)
-        nc.scalar.activation(out=warm[:], in_=warm[:], func=ACT.Silu)
 
         ones = const.tile([P, P], BF16)
         nc.vector.memset(ones[:], 1.0)
@@ -140,36 +139,47 @@ def tile_gatedattentionunit_pa_t_kernel(
 
         w_codes = const.tile([P, PASSES, E], U32, align_bytes=64)
         w_scales = const.tile([P, PASSES, E], U8, align_bytes=64)
-        for c in range(PASSES):
+        w_grouped = {}
+
+        def group_w(c):
+            for n, copy in enumerate((nc.vector.tensor_copy, nc.scalar.copy)):
+                w_grouped[c, n] = w_stage.tile(
+                    [P, N_BANK, 4], BF16, name="w_grouped", align_bytes=64
+                )
+                copy(
+                    out=w_grouped[c, n][:].rearrange("p (n i) j -> p n j i", i=4),
+                    in_=w_raw[:, c, :, n * N_BANK : (n + 1) * N_BANK].rearrange(
+                        "p j (n i) -> p n j i", i=4
+                    ),
+                )
+
+        def quantise_w(c):
             for n in range(E // N_BANK):
                 cols = slice(n * N_BANK, (n + 1) * N_BANK)
-                w_grouped = w_stage.tile([P, N_BANK, 4], BF16, align_bytes=64)
-                nc.vector.tensor_copy(
-                    out=w_grouped[:].rearrange("p (n i) j -> p n j i", i=4),
-                    in_=w_raw[:, c, :, cols].rearrange("p j (n i) -> p n j i", i=4),
-                )
                 nc.vector.quantize_mx(
                     out=w_codes[:, c, cols].bitcast(FP8X4),
                     scales=w_scales[:, c, cols],
-                    in_=w_grouped[:].rearrange("p n j -> p (n j)"),
+                    in_=w_grouped[c, n][:].rearrange("p n j -> p (n j)"),
                 )
 
         sumsq = const.tile([P, TILES], F32)
         meansq = const.tile([P, TILES], F32)
         rnorm = const.tile([P, TILES], F32)
+        xn = {}
         x_banks = {}
         x_codes = {}
         x_scales = {}
         qk_t = {}
         qk_banks = {}
-        group_out = {}
+        grouped = {}
+        z = {}
 
         def x_tile(i):
-            return x_sb[i // T][:, i % T, :]
+            return x_sb[i // RUN][:, i % RUN, :]
 
         def norm(r):
             for i in range(r * RUN, (r + 1) * RUN):
-                squares = front.tile([P, D], BF16)
+                squares = front.tile([P, D], BF16, bufs=2)
                 nc.scalar.activation(
                     out=squares[:],
                     in_=x_tile(i),
@@ -189,19 +199,22 @@ def tile_gatedattentionunit_pa_t_kernel(
                 out=rnorm[:, cols], in0=meansq[:, cols], in1=neg_half[:], op=ALU.pow
             )
 
-        def transpose_x(r):
-            x_banks[r] = []
+        def normalise(r):
             for i in range(r * RUN, (r + 1) * RUN):
-                xn = front.tile([P, D], BF16)
+                xn[i] = front.tile([P, D], BF16, name="xn")
                 nc.vector.tensor_scalar(
-                    out=xn[:],
+                    out=xn[i][:],
                     in0=x_tile(i),
                     scalar1=rnorm[:, i : i + 1],
                     scalar2=g_f32[:],
                     op0=ALU.mult,
                     op1=ALU.mult,
                 )
-                xn_words = xn[:].bitcast(F32)
+
+        def transpose_x(r):
+            x_banks[r] = []
+            for i in range(r * RUN, (r + 1) * RUN):
+                xn_words = xn[i][:].bitcast(F32)
                 bank = psum_t.tile([P, WORD_BLOCKS, P], F32, name="bank_t")
                 for j in range(WORD_BLOCKS):
                     nc.tensor.transpose(
@@ -210,8 +223,10 @@ def tile_gatedattentionunit_pa_t_kernel(
                 x_banks[r].append(bank)
 
         def copy_out_x(r):
-            grouped = front.tile([P, PASSES * RUN_TOKENS * 4], BF16, align_bytes=64)
-            words = grouped[:].bitcast(F32).rearrange(
+            grouped[r] = front.tile(
+                [P, PASSES * RUN_TOKENS * 4], BF16, name="grouped", align_bytes=64
+            )
+            words = grouped[r][:].bitcast(F32).rearrange(
                 "p (c s r u) -> p c s r u", c=PASSES, s=RUN, u=2
             )
             for s, bank in enumerate(x_banks[r]):
@@ -219,9 +234,8 @@ def tile_gatedattentionunit_pa_t_kernel(
                     out=words[:, :, s, :, :],
                     in_=bank[:].rearrange("p (c u) r -> p c r u", u=2),
                 )
-            return grouped
 
-        def quantise_x(r, grouped):
+        def quantise_x(r):
             x_codes[r] = front.tile(
                 [P, PASSES * RUN_TOKENS], U32, name="x_codes", align_bytes=64
             )
@@ -229,7 +243,7 @@ def tile_gatedattentionunit_pa_t_kernel(
                 [P, PASSES * RUN_TOKENS], U8, name="x_scales", align_bytes=64
             )
             nc.vector.quantize_mx(
-                out=x_codes[r][:].bitcast(FP8X4), scales=x_scales[r][:], in_=grouped[:]
+                out=x_codes[r][:].bitcast(FP8X4), scales=x_scales[r][:], in_=grouped[r][:]
             )
 
         def w_operand(c, first, width):
@@ -278,8 +292,7 @@ def tile_gatedattentionunit_pa_t_kernel(
                     )
 
         def project_uv(r):
-            grp, t0 = (r * RUN) // T, (r * RUN) % T
-            z = back.tile([P, RUN, 2 * H], F32)
+            z[r] = back.tile([P, RUN, 2 * H], F32, name="z")
             tail = psum_tail.tile([P, RUN, N_TAIL], F32)
             for s in range(RUN):
                 head = psum_head.tile([P, N_BANK], F32)
@@ -287,29 +300,22 @@ def tile_gatedattentionunit_pa_t_kernel(
                     for c in range(PASSES):
                         mx_pass(out, c, x_operand(r, c, s * P, P), w_operand(c, first, width))
                 nc.vector.tensor_tensor(
-                    out=z[:, s, 0:N_BANK], in0=head[:], in1=uv_bias[:, 0:N_BANK], op=ALU.add
+                    out=z[r][:, s, 0:N_BANK], in0=head[:], in1=uv_bias[:, 0:N_BANK], op=ALU.add
                 )
             nc.vector.tensor_tensor(
-                out=z[:, :, N_BANK : 2 * H],
+                out=z[r][:, :, N_BANK : 2 * H],
                 in0=tail[:],
                 in1=uv_bias[:, N_BANK : 2 * H].unsqueeze(1).to_broadcast([P, RUN, N_TAIL]),
                 op=ALU.add,
             )
-            if t0 == 0:
-                group_out["u"] = outs.tile([P, T, H], F32, name="u_out")
-                group_out["v"] = outs.tile([P, T, H], F32, name="v_out")
-            rows = slice(grp * GROUP, (grp + 1) * GROUP)
-            for dram, sbuf, cols in (
-                (u_rows, group_out["u"], slice(0, H)),
-                (v_rows, group_out["v"], slice(H, 2 * H)),
-            ):
+
+        def finish_uv(r):
+            for dram, first in ((u_rows, 0), (v_rows, H)):
+                uv_out = outs.tile([P, RUN, H], F32, bufs=6)
                 nc.scalar.activation(
-                    out=sbuf[:, t0 : t0 + RUN, :], in_=z[:, :, cols], func=ACT.Silu
+                    out=uv_out[:], in_=z[r][:, :, first : first + H], func=ACT.Silu
                 )
-                if t0 + RUN == T:
-                    nc.sync.dma_start(
-                        out=dram[rows, :].rearrange("(p t) n -> p t n", t=T), in_=sbuf[:]
-                    )
+                nc.sync.dma_start(out=run_rows(dram, r), in_=uv_out[:])
 
         def transpose_qk(r):
             qk_banks[r] = []
@@ -325,33 +331,46 @@ def tile_gatedattentionunit_pa_t_kernel(
                 qk_banks[r].append(bank)
 
         def copy_out_qk(r):
-            grp, t0 = (r * RUN) // T, (r * RUN) % T
-            if t0 == 0:
-                group_out["qk"] = outs.tile([P, 2, T, S], F32, name="qk_out")
-            qk_out = group_out["qk"]
-            nc.vector.tensor_copy(out=qk_out[:, 0, t0 : t0 + RUN, :], in_=qk_banks[r][0][:])
-            nc.scalar.copy(out=qk_out[:, 1, t0 : t0 + RUN, :], in_=qk_banks[r][1][:])
-            if t0 + RUN == T:
-                rows = slice(grp * GROUP, (grp + 1) * GROUP)
-                for a, dram in enumerate((q_rows, k_rows)):
-                    nc.sync.dma_start(
-                        out=dram[rows, :].rearrange("(p t) n -> p t n", t=T),
-                        in_=qk_out[:, a, :, :],
-                    )
+            q_out = outs.tile([P, RUN, S], F32)
+            nc.vector.tensor_copy(out=q_out[:], in_=qk_banks[r][0][:])
+            nc.sync.dma_start(out=run_rows(q_rows, r), in_=q_out[:])
+            k_out = outs.tile([P, RUN, S], F32)
+            if r % 2 == 0:
+                nc.scalar.copy(out=k_out[:], in_=qk_banks[r][1][:])
+            else:
+                nc.vector.tensor_copy(out=k_out[:], in_=qk_banks[r][1][:])
+            nc.sync.dma_start(out=run_rows(k_rows, r), in_=k_out[:])
 
-        for r in range(-2, RUNS + 1):
-            if 0 <= r + 2 < RUNS:
-                norm(r + 2)
-            if 0 <= r + 1 < RUNS:
+        norm(0)
+        group_w(0)
+        normalise(0)
+        transpose_x(0)
+        group_w(1)
+        quantise_w(0)
+        copy_out_x(0)
+        quantise_w(1)
+        quantise_x(0)
+        norm(1)
+        normalise(1)
+        norm(2)
+
+        for r in range(RUNS + 1):
+            if r >= 1:
+                finish_uv(r - 1)
+            if r + 1 < RUNS:
                 transpose_x(r + 1)
-            if 0 <= r - 1 < RUNS:
+            if r >= 1:
                 transpose_qk(r - 1)
-            if 0 <= r + 1 < RUNS:
-                grouped = copy_out_x(r + 1)
-            if 0 <= r - 1 < RUNS:
+            if r + 1 < RUNS:
+                copy_out_x(r + 1)
+            if r >= 1:
                 copy_out_qk(r - 1)
-            if 0 <= r + 1 < RUNS:
-                quantise_x(r + 1, grouped)
-            if 0 <= r < RUNS:
+            if r + 1 < RUNS:
+                quantise_x(r + 1)
+            if r + 2 < RUNS:
+                normalise(r + 2)
+            if r < RUNS:
                 project_base(r)
                 project_uv(r)
+            if r + 3 < RUNS:
+                norm(r + 3)

@@ -276,7 +276,7 @@ def tile_gatedattentionunit_pa_t_kernel(
                         x_operand(r, c, 0, RUN_TOKENS),
                     )
             base_t = back.tile([P, BASE_BLOCKS, RUN_TOKENS], F32)
-            qk_t[r] = back.tile([P, 2, BASE_BLOCKS, RUN_TOKENS], F32, name="qk_t")
+            qk_t[r] = back.tile([P, 2, BASE_BLOCKS, RUN_TOKENS], F32, name="qk_t", bufs=4)
             for b in range(BASE_BLOCKS):
                 nc.scalar.activation(
                     out=base_t[:, b, :], in_=base_ps[:, b, :], func=ACT.Silu, bias=base_bias(b)
@@ -354,17 +354,17 @@ def tile_gatedattentionunit_pa_t_kernel(
         normalise(1)
         norm(2)
 
-        for r in range(RUNS + 1):
-            if r >= 1:
+        for r in range(RUNS + 2):
+            if 1 <= r <= RUNS:
                 finish_uv(r - 1)
             if r + 1 < RUNS:
                 transpose_x(r + 1)
-            if r >= 1:
-                transpose_qk(r - 1)
+            if r >= 2:
+                transpose_qk(r - 2)
             if r + 1 < RUNS:
                 copy_out_x(r + 1)
-            if r >= 1:
-                copy_out_qk(r - 1)
+            if r >= 2:
+                copy_out_qk(r - 2)
             if r + 1 < RUNS:
                 quantise_x(r + 1)
             if r + 2 < RUNS:

@@ -19,7 +19,8 @@ S = 256
 E = 2 * H + S
 EPS = 1e-5
 
-K_PASS = 4 * P
+PACK = 4
+K_PASS = PACK * P
 PASSES = D // K_PASS
 N_BANK = 512
 N_TAIL = 2 * H - N_BANK
@@ -30,6 +31,11 @@ TILES = TOKENS // P
 RUN = 2
 RUN_TOKENS = RUN * P
 RUNS = TILES // RUN
+
+BIAS_ROW = 0
+GAMMA_ROW = BIAS_ROW + BASE_BLOCKS
+BETA_ROW = GAMMA_ROW + 2 * BASE_BLOCKS
+CONST_ROWS = BETA_ROW + 2 * BASE_BLOCKS
 
 FLOPS = 2 * TOKENS * D * E
 
@@ -67,37 +73,46 @@ def tile_gatedattentionunit_pa_t_kernel(
             nc.sync.dma_start(out=x_run[:], in_=run_rows(x_rows, r))
             return x_run
 
+        w_raw = const.tile([P, PASSES, PACK, E], BF16)
+
+        def load_w(c):
+            nc.sync.dma_start(
+                out=w_raw[:, c, :, :].rearrange("p (w e) n -> p w e n", e=2),
+                in_=W_uv[c * K_PASS : (c + 1) * K_PASS, :].rearrange(
+                    "(w p e) n -> p w e n", w=2, e=2
+                ),
+            )
+
+        x_sb = [load_x(0)]
+        load_w(0)
+        x_sb.append(load_x(1))
+        load_w(1)
+        for r in range(2, RUNS):
+            x_sb.append(load_x(r))
+
+        g_bf = const.tile([P, 1], BF16)
+        nc.scalar.dma_start(out=g_bf[:], in_=g.partition_broadcast(P))
+        uv_bias_row = const.tile([P, 2 * H], BF16)
+        nc.vector.memset(uv_bias_row[:], 0.0)
+        nc.scalar.dma_start(out=uv_bias_row[0:1, :], in_=b_uv[0 : 2 * H].unsqueeze(0))
+        base_rows = const.tile([P, P], BF16)
+        nc.vector.memset(base_rows[:], 0.0)
+        nc.scalar.dma_start(
+            out=base_rows[BIAS_ROW:GAMMA_ROW, :],
+            in_=b_uv[2 * H : E].rearrange("(b n) -> b n", n=P),
+        )
+        nc.scalar.dma_start(
+            out=base_rows[GAMMA_ROW:BETA_ROW, :],
+            in_=gamma.rearrange("a (b n) -> (a b) n", n=P),
+        )
+        nc.scalar.dma_start(
+            out=base_rows[BETA_ROW:CONST_ROWS, :],
+            in_=beta.rearrange("a (b n) -> (a b) n", n=P),
+        )
+
         warm = const.tile([P, 1], F32)
         nc.vector.memset(warm[:], 0.0)
         nc.scalar.activation(out=warm[:], in_=warm[:], func=ACT.Silu)
-
-        g_bf = const.tile([P, 1], BF16)
-        nc.sync.dma_start(out=g_bf[:], in_=g.partition_broadcast(P))
-        uv_bias_row = const.tile([P, 2 * H], BF16)
-        nc.vector.memset(uv_bias_row[:], 0.0)
-        nc.sync.dma_start(out=uv_bias_row[0:1, :], in_=b_uv[0 : 2 * H].unsqueeze(0))
-        base_rows = const.tile([P, P], BF16)
-        nc.vector.memset(base_rows[:], 0.0)
-        nc.sync.dma_start(
-            out=base_rows[0:2, :], in_=b_uv[2 * H : E].rearrange("(b n) -> b n", n=P)
-        )
-        nc.sync.dma_start(
-            out=base_rows[2:6, :], in_=gamma.rearrange("a (b n) -> (a b) n", n=P)
-        )
-        nc.sync.dma_start(
-            out=base_rows[6:10, :], in_=beta.rearrange("a (b n) -> (a b) n", n=P)
-        )
-        x_sb = [load_x(0)]
-        w_raw = const.tile([P, PASSES, 4, E], BF16)
-        for c in range(PASSES):
-            nc.sync.dma_start(
-                out=w_raw[:, c, :, :].rearrange("p (u e) n -> p u e n", e=2),
-                in_=W_uv[c * K_PASS : (c + 1) * K_PASS, :].rearrange(
-                    "(u p e) n -> p u e n", u=2, e=2
-                ),
-            )
-        for r in range(1, RUNS):
-            x_sb.append(load_x(r))
 
         ident = const.tile([P, P], F32)
         make_identity(nc, ident[:])
@@ -125,41 +140,36 @@ def tile_gatedattentionunit_pa_t_kernel(
             )
         base_cols_ps = psum_t.tile([P, P], BF16, name="bank_t")
         nc.tensor.transpose(base_cols_ps[:], base_rows[:], ident_bf[:])
-        base_cols = const.tile([P, 10], F32)
-        nc.vector.tensor_copy(out=base_cols[:], in_=base_cols_ps[:, 0:10])
+        base_cols = const.tile([P, CONST_ROWS], F32)
+        nc.vector.tensor_copy(out=base_cols[:], in_=base_cols_ps[:, 0:CONST_ROWS])
 
-        def base_bias(b):
-            return base_cols[:, b : b + 1]
-
-        def base_gamma(a, b):
-            return base_cols[:, 2 + 2 * a + b : 3 + 2 * a + b]
-
-        def base_beta(a, b):
-            return base_cols[:, 6 + 2 * a + b : 7 + 2 * a + b]
+        def base_const(first_row, a, b):
+            row = first_row + a * BASE_BLOCKS + b
+            return base_cols[:, row : row + 1]
 
         w_codes = const.tile([P, PASSES, E], U32, align_bytes=64)
         w_scales = const.tile([P, PASSES, E], U8, align_bytes=64)
         w_grouped = {}
 
         def group_w(c):
-            for n, copy in enumerate((nc.vector.tensor_copy, nc.scalar.copy)):
-                w_grouped[c, n] = w_stage.tile(
-                    [P, N_BANK, 4], BF16, name="w_grouped", align_bytes=64
+            for half, copy in enumerate((nc.vector.tensor_copy, nc.scalar.copy)):
+                w_grouped[c, half] = w_stage.tile(
+                    [P, N_BANK, PACK], BF16, name="w_grouped", align_bytes=64
                 )
                 copy(
-                    out=w_grouped[c, n][:].rearrange("p (n i) j -> p n j i", i=4),
-                    in_=w_raw[:, c, :, n * N_BANK : (n + 1) * N_BANK].rearrange(
-                        "p j (n i) -> p n j i", i=4
+                    out=w_grouped[c, half][:].rearrange("p (n m) j -> p n j m", m=4),
+                    in_=w_raw[:, c, :, half * N_BANK : (half + 1) * N_BANK].rearrange(
+                        "p j (n m) -> p n j m", m=4
                     ),
                 )
 
         def quantise_w(c):
-            for n in range(E // N_BANK):
-                cols = slice(n * N_BANK, (n + 1) * N_BANK)
+            for half in range(E // N_BANK):
+                cols = slice(half * N_BANK, (half + 1) * N_BANK)
                 nc.vector.quantize_mx(
                     out=w_codes[:, c, cols].bitcast(FP8X4),
                     scales=w_scales[:, c, cols],
-                    in_=w_grouped[c, n][:].rearrange("p n j -> p (n j)"),
+                    in_=w_grouped[c, half][:].rearrange("p n j -> p (n j)"),
                 )
 
         sumsq = const.tile([P, TILES], F32)
@@ -216,23 +226,23 @@ def tile_gatedattentionunit_pa_t_kernel(
             for i in range(r * RUN, (r + 1) * RUN):
                 xn_words = xn[i][:].bitcast(F32)
                 bank = psum_t.tile([P, WORD_BLOCKS, P], F32, name="bank_t")
-                for j in range(WORD_BLOCKS):
+                for block in range(WORD_BLOCKS):
                     nc.tensor.transpose(
-                        bank[:, j, :], xn_words[:, j * P : (j + 1) * P], ident[:]
+                        bank[:, block, :], xn_words[:, block * P : (block + 1) * P], ident[:]
                     )
                 x_banks[r].append(bank)
 
         def copy_out_x(r):
             grouped[r] = front.tile(
-                [P, PASSES * RUN_TOKENS * 4], BF16, name="grouped", align_bytes=64
+                [P, PASSES * RUN_TOKENS * PACK], BF16, name="grouped", align_bytes=64
             )
             words = grouped[r][:].bitcast(F32).rearrange(
-                "p (c s r u) -> p c s r u", c=PASSES, s=RUN, u=2
+                "p (c s t w) -> p c s t w", c=PASSES, s=RUN, w=2
             )
             for s, bank in enumerate(x_banks[r]):
                 nc.vector.tensor_copy(
                     out=words[:, :, s, :, :],
-                    in_=bank[:].rearrange("p (c u) r -> p c r u", u=2),
+                    in_=bank[:].rearrange("p (c w) t -> p c t w", w=2),
                 )
 
         def quantise_x(r):
@@ -279,14 +289,17 @@ def tile_gatedattentionunit_pa_t_kernel(
             qk_t[r] = back.tile([P, 2, BASE_BLOCKS, RUN_TOKENS], F32, name="qk_t", bufs=4)
             for b in range(BASE_BLOCKS):
                 nc.scalar.activation(
-                    out=base_t[:, b, :], in_=base_ps[:, b, :], func=ACT.Silu, bias=base_bias(b)
+                    out=base_t[:, b, :],
+                    in_=base_ps[:, b, :],
+                    func=ACT.Silu,
+                    bias=base_const(BIAS_ROW, 0, b),
                 )
                 for a in range(2):
                     nc.gpsimd.tensor_scalar(
                         out=qk_t[r][:, a, b, :],
                         in0=base_t[:, b, :],
-                        scalar1=base_gamma(a, b),
-                        scalar2=base_beta(a, b),
+                        scalar1=base_const(GAMMA_ROW, a, b),
+                        scalar2=base_const(BETA_ROW, a, b),
                         op0=ALU.mult,
                         op1=ALU.add,
                     )
@@ -345,13 +358,13 @@ def tile_gatedattentionunit_pa_t_kernel(
         group_w(0)
         normalise(0)
         transpose_x(0)
-        group_w(1)
         quantise_w(0)
-        copy_out_x(0)
-        quantise_w(1)
-        quantise_x(0)
         norm(1)
+        group_w(1)
+        copy_out_x(0)
         normalise(1)
+        quantise_x(0)
+        quantise_w(1)
         norm(2)
 
         for r in range(RUNS + 2):

from contextlib import ExitStack

import concourse.mybir as mybir
from concourse.masks import make_identity

F32 = mybir.dt.float32
BF16 = mybir.dt.bfloat16
U32 = mybir.dt.uint32
U8 = mybir.dt.uint8
FP8X4 = mybir.dt.float8_e4m3fn_x4
ACT = mybir.ActivationFunctionType
ALU = mybir.AluOpType

P = 128
TOKENS = 4 * 1024
D = 1024
H = 384
S = 256
E = 2 * H + S
EPS = 1e-5

PACK = 4
K_PASS = PACK * P
PASSES = D // K_PASS
N_BANK = 512
N_TAIL = 2 * H - N_BANK
WORD_BLOCKS = D // 2 // P
BASE_BLOCKS = S // P

TILES = TOKENS // P
RUN = 2
RUN_TOKENS = RUN * P
RUNS = TILES // RUN

BIAS_ROW = 0
GAMMA_ROW = BIAS_ROW + BASE_BLOCKS
BETA_ROW = GAMMA_ROW + 2 * BASE_BLOCKS
CONST_ROWS = BETA_ROW + 2 * BASE_BLOCKS

FLOPS = 2 * TOKENS * D * E


def tile_gatedattentionunit_pa_t_kernel(
    tc, x, g, W_uv, b_uv, gamma, beta, out_0, out_1, out_2, out_3
):
    nc = tc.nc
    x_rows = x.flatten_outer_dims()
    u_rows = out_0.flatten_outer_dims()
    v_rows = out_1.flatten_outer_dims()
    q_rows = out_2.flatten_outer_dims()
    k_rows = out_3.flatten_outer_dims()

    with ExitStack() as stack:
        const = stack.enter_context(tc.tile_pool(name="const", bufs=1))
        x_pool = stack.enter_context(tc.tile_pool(name="x_pool", bufs=1))
        w_stage = stack.enter_context(tc.tile_pool(name="w_stage", bufs=4))
        front = stack.enter_context(tc.tile_pool(name="front", bufs=4))
        back = stack.enter_context(tc.tile_pool(name="back", bufs=3))
        outs = stack.enter_context(tc.tile_pool(name="outs", bufs=4))
        psum_t = stack.enter_context(tc.psum_pool(name="psum_t", bufs=4))
        psum_head = stack.enter_context(tc.psum_pool(name="psum_head", bufs=2))
        psum_tail = stack.enter_context(tc.psum_pool(name="psum_tail", bufs=1))
        psum_base = stack.enter_context(tc.psum_pool(name="psum_base", bufs=1))
        stack.enter_context(tc.manual_schedule())

        def run_rows(dram, r):
            return dram[r * RUN_TOKENS : (r + 1) * RUN_TOKENS, :].rearrange(
                "(p s) n -> p s n", s=RUN
            )

        def load_x(r):
            x_run = x_pool.tile([P, RUN, D], BF16, name="x_run%d" % r)
            nc.sync.dma_start(out=x_run[:], in_=run_rows(x_rows, r))
            return x_run

        w_raw = const.tile([P, PASSES, PACK, E], BF16)

        def load_w(c):
            nc.sync.dma_start(
                out=w_raw[:, c, :, :].rearrange("p (w e) n -> p w e n", e=2),
                in_=W_uv[c * K_PASS : (c + 1) * K_PASS, :].rearrange(
                    "(w p e) n -> p w e n", w=2, e=2
                ),
            )

        x_sb = [load_x(0)]
        load_w(0)
        x_sb.append(load_x(1))
        load_w(1)
        for r in range(2, RUNS):
            x_sb.append(load_x(r))

        g_bf = const.tile([P, 1], BF16)
        nc.scalar.dma_start(out=g_bf[:], in_=g.partition_broadcast(P))
        uv_bias_row = const.tile([P, 2 * H], BF16)
        nc.vector.memset(uv_bias_row[:], 0.0)
        nc.scalar.dma_start(out=uv_bias_row[0:1, :], in_=b_uv[0 : 2 * H].unsqueeze(0))
        base_rows = const.tile([P, P], BF16)
        nc.vector.memset(base_rows[:], 0.0)
        nc.scalar.dma_start(
            out=base_rows[BIAS_ROW:GAMMA_ROW, :],
            in_=b_uv[2 * H : E].rearrange("(b n) -> b n", n=P),
        )
        nc.scalar.dma_start(
            out=base_rows[GAMMA_ROW:BETA_ROW, :],
            in_=gamma.rearrange("a (b n) -> (a b) n", n=P),
        )
        nc.scalar.dma_start(
            out=base_rows[BETA_ROW:CONST_ROWS, :],
            in_=beta.rearrange("a (b n) -> (a b) n", n=P),
        )

        warm = const.tile([P, 1], F32)
        nc.vector.memset(warm[:], 0.0)
        nc.scalar.activation(out=warm[:], in_=warm[:], func=ACT.Silu)

        ident = const.tile([P, P], F32)
        make_identity(nc, ident[:])
        ident_bf = const.tile([P, P], BF16)
        make_identity(nc, ident_bf[:])
        neg_half = const.tile([P, RUN], F32)
        nc.gpsimd.memset(neg_half[:], -0.5)
        g_f32 = const.tile([P, 1], F32)
        nc.vector.tensor_copy(out=g_f32[:], in_=g_bf[:])

        ones = const.tile([P, P], BF16)
        nc.vector.memset(ones[:], 1.0)
        uv_bias = const.tile([P, 2 * H], F32)
        for first, width in ((0, N_BANK), (N_BANK, N_TAIL)):
            spread = psum_head.tile([P, N_BANK], F32, name="head")
            nc.tensor.matmul(
                out=spread[:, 0:width],
                lhsT=ones[:],
                rhs=uv_bias_row[:, first : first + width],
                start=True,
                stop=True,
            )
            nc.vector.tensor_copy(
                out=uv_bias[:, first : first + width], in_=spread[:, 0:width]
            )
        base_cols_ps = psum_t.tile([P, P], BF16, name="bank_t")
        nc.tensor.transpose(base_cols_ps[:], base_rows[:], ident_bf[:])
        base_cols = const.tile([P, CONST_ROWS], F32)
        nc.vector.tensor_copy(out=base_cols[:], in_=base_cols_ps[:, 0:CONST_ROWS])

        def base_const(first_row, a, b):
            row = first_row + a * BASE_BLOCKS + b
            return base_cols[:, row : row + 1]

        w_codes = const.tile([P, PASSES, E], U32, align_bytes=64)
        w_scales = const.tile([P, PASSES, E], U8, align_bytes=64)
        w_grouped = {}

        def group_w(c):
            for half, copy in enumerate((nc.vector.tensor_copy, nc.scalar.copy)):
                w_grouped[c, half] = w_stage.tile(
                    [P, N_BANK, PACK], BF16, name="w_grouped", align_bytes=64
                )
                copy(
                    out=w_grouped[c, half][:].rearrange("p (n m) j -> p n j m", m=4),
                    in_=w_raw[:, c, :, half * N_BANK : (half + 1) * N_BANK].rearrange(
                        "p j (n m) -> p n j m", m=4
                    ),
                )

        def quantise_w(c):
            for half in range(E // N_BANK):
                cols = slice(half * N_BANK, (half + 1) * N_BANK)
                nc.vector.quantize_mx(
                    out=w_codes[:, c, cols].bitcast(FP8X4),
                    scales=w_scales[:, c, cols],
                    in_=w_grouped[c, half][:].rearrange("p n j -> p (n j)"),
                )

        sumsq = const.tile([P, TILES], F32)
        meansq = const.tile([P, TILES], F32)
        rnorm = const.tile([P, TILES], F32)
        xn = {}
        x_banks = {}
        x_codes = {}
        x_scales = {}
        qk_t = {}
        qk_banks = {}
        grouped = {}
        z = {}

        def x_tile(i):
            return x_sb[i // RUN][:, i % RUN, :]

        def norm(r):
            for i in range(r * RUN, (r + 1) * RUN):
                squares = front.tile([P, D], BF16, bufs=2)
                nc.scalar.activation(
                    out=squares[:],
                    in_=x_tile(i),
                    func=ACT.Square,
                    accum_out=sumsq[:, i : i + 1],
                )
            cols = slice(r * RUN, (r + 1) * RUN)
            nc.gpsimd.tensor_scalar(
                out=meansq[:, cols],
                in0=sumsq[:, cols],
                scalar1=1.0 / D,
                scalar2=EPS * EPS,
                op0=ALU.mult,
                op1=ALU.max,
            )
            nc.gpsimd.tensor_tensor(
                out=rnorm[:, cols], in0=meansq[:, cols], in1=neg_half[:], op=ALU.pow
            )

        def normalise(r):
            for i in range(r * RUN, (r + 1) * RUN):
                xn[i] = front.tile([P, D], BF16, name="xn")
                nc.vector.tensor_scalar(
                    out=xn[i][:],
                    in0=x_tile(i),
                    scalar1=rnorm[:, i : i + 1],
                    scalar2=g_f32[:],
                    op0=ALU.mult,
                    op1=ALU.mult,
                )

        def transpose_x(r):
            x_banks[r] = []
            for i in range(r * RUN, (r + 1) * RUN):
                xn_words = xn[i][:].bitcast(F32)
                bank = psum_t.tile([P, WORD_BLOCKS, P], F32, name="bank_t")
                for block in range(WORD_BLOCKS):
                    nc.tensor.transpose(
                        bank[:, block, :], xn_words[:, block * P : (block + 1) * P], ident[:]
                    )
                x_banks[r].append(bank)

        def copy_out_x(r):
            grouped[r] = front.tile(
                [P, PASSES * RUN_TOKENS * PACK], BF16, name="grouped", align_bytes=64
            )
            words = grouped[r][:].bitcast(F32).rearrange(
                "p (c s t w) -> p c s t w", c=PASSES, s=RUN, w=2
            )
            for s, bank in enumerate(x_banks[r]):
                nc.vector.tensor_copy(
                    out=words[:, :, s, :, :],
                    in_=bank[:].rearrange("p (c w) t -> p c t w", w=2),
                )

        def quantise_x(r):
            x_codes[r] = front.tile(
                [P, PASSES * RUN_TOKENS], U32, name="x_codes", align_bytes=64
            )
            x_scales[r] = front.tile(
                [P, PASSES * RUN_TOKENS], U8, name="x_scales", align_bytes=64
            )
            nc.vector.quantize_mx(
                out=x_codes[r][:].bitcast(FP8X4), scales=x_scales[r][:], in_=grouped[r][:]
            )

        def w_operand(c, first, width):
            cols = slice(first, first + width)
            return w_codes[:, c, cols], w_scales[:, c, cols]

        def x_operand(r, c, first, width):
            cols = slice(c * RUN_TOKENS + first, c * RUN_TOKENS + first + width)
            return x_codes[r][:, cols], x_scales[r][:, cols]

        def mx_pass(out, c, stationary, moving):
            nc.tensor.matmul_mx(
                out=out,
                lhsT=stationary[0].bitcast(FP8X4),
                lhsT_scale=stationary[1],
                rhs=moving[0].bitcast(FP8X4),
                rhs_scale=moving[1],
                start=(c == 0),
                stop=(c == PASSES - 1),
            )

        def project_base(r):
            base_ps = psum_base.tile([P, BASE_BLOCKS, RUN_TOKENS], F32)
            for b in range(BASE_BLOCKS):
                for c in range(PASSES):
                    mx_pass(
                        base_ps[:, b, :],
                        c,
                        w_operand(c, 2 * H + b * P, P),
                        x_operand(r, c, 0, RUN_TOKENS),
                    )
            base_t = back.tile([P, BASE_BLOCKS, RUN_TOKENS], F32)
            qk_t[r] = back.tile([P, 2, BASE_BLOCKS, RUN_TOKENS], F32, name="qk_t", bufs=4)
            for b in range(BASE_BLOCKS):
                nc.scalar.activation(
                    out=base_t[:, b, :],
                    in_=base_ps[:, b, :],
                    func=ACT.Silu,
                    bias=base_const(BIAS_ROW, 0, b),
                )
                for a in range(2):
                    nc.gpsimd.tensor_scalar(
                        out=qk_t[r][:, a, b, :],
                        in0=base_t[:, b, :],
                        scalar1=base_const(GAMMA_ROW, a, b),
                        scalar2=base_const(BETA_ROW, a, b),
                        op0=ALU.mult,
                        op1=ALU.add,
                    )

        def project_uv(r):
            z[r] = back.tile([P, RUN, 2 * H], F32, name="z")
            tail = psum_tail.tile([P, RUN, N_TAIL], F32)
            for s in range(RUN):
                head = psum_head.tile([P, N_BANK], F32)
                for out, first, width in ((head[:], 0, N_BANK), (tail[:, s, :], N_BANK, N_TAIL)):
                    for c in range(PASSES):
                        mx_pass(out, c, x_operand(r, c, s * P, P), w_operand(c, first, width))
                nc.vector.tensor_tensor(
                    out=z[r][:, s, 0:N_BANK], in0=head[:], in1=uv_bias[:, 0:N_BANK], op=ALU.add
                )
            nc.vector.tensor_tensor(
                out=z[r][:, :, N_BANK : 2 * H],
                in0=tail[:],
                in1=uv_bias[:, N_BANK : 2 * H].unsqueeze(1).to_broadcast([P, RUN, N_TAIL]),
                op=ALU.add,
            )

        def finish_uv(r):
            for dram, first in ((u_rows, 0), (v_rows, H)):
                uv_out = outs.tile([P, RUN, H], F32, bufs=6)
                nc.scalar.activation(
                    out=uv_out[:], in_=z[r][:, :, first : first + H], func=ACT.Silu
                )
                nc.sync.dma_start(out=run_rows(dram, r), in_=uv_out[:])

        def transpose_qk(r):
            qk_banks[r] = []
            for a in range(2):
                bank = psum_t.tile([P, RUN, S], F32, name="bank_t")
                for s in range(RUN):
                    for b in range(BASE_BLOCKS):
                        nc.tensor.transpose(
                            bank[:, s, b * P : (b + 1) * P],
                            qk_t[r][:, a, b, s * P : (s + 1) * P],
                            ident[:],
                        )
                qk_banks[r].append(bank)

        def copy_out_qk(r):
            q_out = outs.tile([P, RUN, S], F32)
            nc.vector.tensor_copy(out=q_out[:], in_=qk_banks[r][0][:])
            nc.sync.dma_start(out=run_rows(q_rows, r), in_=q_out[:])
            k_out = outs.tile([P, RUN, S], F32)
            if r % 2 == 0:
                nc.scalar.copy(out=k_out[:], in_=qk_banks[r][1][:])
            else:
                nc.vector.tensor_copy(out=k_out[:], in_=qk_banks[r][1][:])
            nc.sync.dma_start(out=run_rows(k_rows, r), in_=k_out[:])

        norm(0)
        group_w(0)
        normalise(0)
        transpose_x(0)
        quantise_w(0)
        norm(1)
        group_w(1)
        copy_out_x(0)
        normalise(1)
        quantise_x(0)
        quantise_w(1)
        norm(2)

        for r in range(RUNS + 2):
            if 1 <= r <= RUNS:
                finish_uv(r - 1)
            if r + 1 < RUNS:
                transpose_x(r + 1)
            if r >= 2:
                transpose_qk(r - 2)
            if r + 1 < RUNS:
                copy_out_x(r + 1)
            if r >= 2:
                copy_out_qk(r - 2)
            if r + 1 < RUNS:
                quantise_x(r + 1)
            if r + 2 < RUNS:
                normalise(r + 2)
            if r < RUNS:
                project_base(r)
                project_uv(r)
            if r + 3 < RUNS:
                norm(r + 3)
